import numpy as np
import ml_dtypes


def mxq(x, axis, fmt="e4m3"):
    dtype, down = {"e4m3": (ml_dtypes.float8_e4m3fn, 7), "e5m2": (ml_dtypes.float8_e5m2, 14)}[fmt]
    v = np.moveaxis(np.asarray(x, np.float32).astype(ml_dtypes.bfloat16).astype(np.float64), axis, -1)
    blocks = v.reshape(v.shape[:-1] + (-1, 32))
    amax = np.abs(blocks).max(-1, keepdims=True)
    byte = np.maximum(np.where(amax > 0, np.frexp(amax)[1] - 1 + 127, 0) - down, 1)
    scale = np.exp2(byte - 127.0)
    codes = (blocks / scale).astype(np.float32).astype(dtype).astype(np.float64)
    return np.moveaxis((codes * scale).reshape(v.shape), -1, axis)


WIDE = False


def mx_kscale(k):
    if not WIDE:
        return np.ones(k)
    levels = np.array([10, -10, 5, -5, 0])
    a = np.random.permutation(np.resize(levels, k // 512 * 4)).reshape(k // 512, 4)
    idx = np.arange(k)
    return np.exp2(a[idx // 512, idx % 128 // 32])


BF16 = ml_dtypes.bfloat16


def bf(x):
    return np.asarray(x, np.float32).astype(BF16)


def f64(x):
    return np.asarray(x).astype(np.float64)


B, T, D, H, DH, DFF = 4, 2048, 1024, 4, 32, 4096
HD = H * DH
EPS = 1e-5


def layer_norm(x, w):
    mu = x.mean(-1, keepdims=True)
    var = ((x - mu) ** 2).mean(-1, keepdims=True)
    return (x - mu) * (1.0 / np.sqrt(var + EPS)) * w


def setup_inputs():
    s = mx_kscale(D)
    spread = 0.5 + np.random.random((B, T, 1))
    shift = 0.5 * np.random.standard_normal((B, T, 1))
    return {"x": bf(np.random.standard_normal((B, T, D)) * spread + shift),
            "ln1_w": bf((1.0 + 0.1 * np.random.standard_normal(D)) * s),
            "qkv_w": bf(np.random.standard_normal((3 * HD, D)) / np.sqrt(D) / s[None, :])}


def reference(x, ln1_w, qkv_w):
    h = layer_norm(f64(x), f64(ln1_w))
    qkv = mxq(h, 2, "e4m3") @ mxq(f64(qkv_w), 1, "e4m3").T
    qkv = qkv.reshape(B, T, 3, H, DH)
    q = qkv[:, :, 0].transpose(0, 2, 1, 3)
    k = qkv[:, :, 1].transpose(0, 2, 1, 3)
    v = qkv[:, :, 2].transpose(0, 2, 1, 3)
    return q, k, v

@@ -1,0 +1,280 @@
+from contextlib import ExitStack
+
+import concourse.mybir as mybir
+from concourse.masks import make_identity
+
+BF16 = mybir.dt.bfloat16
+F32 = mybir.dt.float32
+U32 = mybir.dt.uint32
+U8 = mybir.dt.uint8
+FP8X4 = mybir.dt.float8_e4m3fn_x4
+ALU = mybir.AluOpType
+ACT = mybir.ActivationFunctionType
+
+BATCH, TOKENS, D = 4, 2048, 1024
+HEADS, DH = 4, 32
+C = 3 * HEADS * DH
+EPS = 1e-5
+
+P = 128
+PACK = 4
+K_PASS = P * PACK
+PASSES = D // K_PASS
+N_PAD = 512
+
+ROWS = TOKENS // P
+CHUNK = 4
+TILES = BATCH * ROWS
+CHUNKS = TILES // CHUNK
+CHUNKS_PER_BATCH = ROWS // CHUNK
+PREFETCH = 2
+
+SQUARES_LAG = 4
+RSTD_LAG = 5
+NORMALISE_LAG = 9
+TRANSPOSE_LAG = 11
+GAIN_LAG = 12
+QUANTISE_LAG = 13
+MATMUL_LAG = 14
+COPY_OUT_LAG = 15
+
+FLOPS = 2 * BATCH * TOKENS * D * C
+
+
+def tile_traceableencoderlayer_pa_t_kernel(tc, x, ln1_w, qkv_w, out_0, out_1, out_2):
+    nc = tc.nc
+    outs = (out_0, out_1, out_2)
+
+    with ExitStack() as ctx:
+        const = ctx.enter_context(tc.tile_pool(name="const", bufs=1))
+        x_pool = ctx.enter_context(tc.tile_pool(name="x_pool", bufs=6))
+        stats = ctx.enter_context(tc.tile_pool(name="stats", bufs=4))
+        scrap = ctx.enter_context(tc.tile_pool(name="scrap", bufs=2))
+        y_pool = ctx.enter_context(tc.tile_pool(name="y_pool", bufs=4))
+        mx_pool = ctx.enter_context(tc.tile_pool(name="mx_pool", bufs=3))
+        out_pool = ctx.enter_context(tc.tile_pool(name="out_pool", bufs=3))
+        psum_t = ctx.enter_context(tc.psum_pool(name="psum_t", bufs=4))
+        psum_o = ctx.enter_context(tc.psum_pool(name="psum_o", bufs=3))
+        ctx.enter_context(tc.manual_schedule())
+
+        x_tiles, sums, neg_mean, sq_sums, rstd = {}, {}, {}, {}, {}
+        y_tiles, turned, grouped, codes, scales, acc, out_tiles = {}, {}, {}, {}, {}, {}, {}
+
+        def load(c):
+            b, q = divmod(c, CHUNKS_PER_BATCH)
+            x_tiles[c] = x_pool.tile([P, CHUNK, D], BF16, name="x_chunk")
+            rows = x[b].rearrange("(p s) k -> p s k", s=ROWS)
+            nc.sync.dma_start(out=x_tiles[c][:], in_=rows[:, q * CHUNK : (q + 1) * CHUNK, :])
+
+        w_raw = const.tile([P, C // P, D], BF16, name="w_raw")
+        nc.sync.dma_start(out=w_raw[:], in_=qkv_w.rearrange("(a p) k -> p a k", p=P))
+        gain_rows = const.tile([P, P], BF16, name="gain_rows")
+        nc.vector.memset(gain_rows[:], 0.0)
+        nc.sync.dma_start(out=gain_rows[0 : D // P, :], in_=ln1_w.rearrange("(j p) -> j p", p=P))
+        for c in range(PREFETCH):
+            load(c)
+
+        ident_bf = const.tile([P, P], BF16, name="ident_bf")
+        make_identity(nc, ident_bf[:])
+        ident_f32 = const.tile([P, P], F32, name="ident_f32")
+        make_identity(nc, ident_f32[:])
+        eps = const.tile([P, 1], F32, name="eps")
+        nc.vector.memset(eps[:], EPS)
+
+        w_grouped = const.tile([P, PASSES, N_PAD, PACK], BF16, name="w_grouped", align_bytes=64)
+        nc.vector.memset(w_grouped[:], 0.0)
+        w_codes = const.tile([P, PASSES, N_PAD], U32, name="w_codes", align_bytes=64)
+        w_scales = const.tile([P, PASSES, N_PAD], U8, name="w_scales", align_bytes=64)
+        gain_cols = const.tile([P, D // P], F32, name="gain_cols")
+
+        for a in range(C // P):
+            w_turned = psum_t.tile([P, PASSES, PACK, P], BF16, name="w_turned", tag="turned")
+            for g in range(PASSES):
+                for t in range(PACK):
+                    k0 = g * K_PASS + t * P
+                    nc.tensor.transpose(w_turned[:, g, t, :], w_raw[:, a, k0 : k0 + P], ident_bf[:])
+            nc.scalar.copy(
+                out=w_grouped[:, :, a * P : (a + 1) * P, :],
+                in_=w_turned[:].rearrange("p g t c -> p g c t"),
+            )
+        gain_turned = psum_t.tile([P, P], BF16, name="gain_turned", tag="turned")
+        nc.tensor.transpose(gain_turned[:], gain_rows[:], ident_bf[:])
+        nc.scalar.copy(out=gain_cols[:], in_=gain_turned[:, 0 : D // P])
+
+        def quantise_weights():
+            nc.vector.quantize_mx(
+                out=w_codes[:].rearrange("p g c -> p (g c)").bitcast(FP8X4),
+                scales=w_scales[:].rearrange("p g c -> p (g c)"),
+                in_=w_grouped[:].rearrange("p g c t -> p (g c t)"),
+            )
+
+        def row_sum(i):
+            c, j = divmod(i, CHUNK)
+            if j == 0:
+                sums[c] = stats.tile([P, CHUNK], F32, name="sums")
+            unread = scrap.tile([P, D], BF16, name="unread_v")
+            nc.vector.tensor_scalar(
+                out=unread[:],
+                in0=x_tiles[c][:, j, :],
+                scalar1=1.0,
+                scalar2=None,
+                op0=ALU.mult,
+                op1=ALU.add,
+                accum_out=sums[c][:, j : j + 1],
+            )
+
+        def mean(c):
+            neg_mean[c] = stats.tile([P, CHUNK], F32, name="neg_mean")
+            nc.vector.tensor_scalar_mul(out=neg_mean[c][:], in0=sums[c][:], scalar1=-1.0 / D)
+
+        def squares(i):
+            c, j = divmod(i, CHUNK)
+            if j == 0:
+                sq_sums[c] = stats.tile([P, CHUNK], F32, name="sq_sums")
+            unread = scrap.tile([P, D], BF16, name="unread_s")
+            nc.scalar.activation(
+                out=unread[:],
+                in_=x_tiles[c][:, j, :],
+                func=ACT.Square,
+                bias=neg_mean[c][:, j : j + 1],
+                scale=1.0,
+                accum_out=sq_sums[c][:, j : j + 1],
+            )
+
+        std = {}
+
+        def deviation(c):
+            std[c] = stats.tile([P, CHUNK], F32, name="std")
+            nc.scalar.activation(
+                out=std[c][:], in_=sq_sums[c][:], func=ACT.Sqrt, bias=eps[:, 0:1], scale=1.0 / D
+            )
+
+        def inverse_deviation(c):
+            rstd[c] = stats.tile([P, CHUNK], F32, name="rstd")
+            nc.vector.reciprocal(out=rstd[c][:], in_=std[c][:])
+
+        def normalise(i):
+            c, j = divmod(i, CHUNK)
+            y_tiles[i] = y_pool.tile([P, D], F32, name="y")
+            nc.gpsimd.tensor_scalar(
+                out=y_tiles[i][:],
+                in0=x_tiles[c][:, j, :],
+                scalar1=neg_mean[c][:, j : j + 1],
+                scalar2=rstd[c][:, j : j + 1],
+                op0=ALU.add,
+                op1=ALU.mult,
+            )
+
+        def transpose(i):
+            turned[i] = []
+            for g in range(PASSES):
+                bank = psum_t.tile([P, PACK, P], F32, name="turned")
+                for t in range(PACK):
+                    k0 = g * K_PASS + t * P
+                    nc.tensor.transpose(bank[:, t, :], y_tiles[i][:, k0 : k0 + P], ident_f32[:])
+                turned[i].append(bank)
+
+        def gain(i):
+            grouped[i] = mx_pool.tile([P, PASSES, P, PACK], BF16, name="grouped", align_bytes=64)
+            for g in range(PASSES):
+                nc.vector.tensor_tensor(
+                    out=grouped[i][:, g, :, :],
+                    in0=turned[i][g][:].rearrange("p t r -> p r t"),
+                    in1=gain_cols[:, g * PACK : (g + 1) * PACK].unsqueeze(1).to_broadcast([P, P, PACK]),
+                    op=ALU.mult,
+                )
+
+        def quantise(i):
+            codes[i] = mx_pool.tile([P, PASSES, P], U32, name="codes", align_bytes=64)
+            scales[i] = mx_pool.tile([P, PASSES, P], U8, name="scales", align_bytes=64)
+            nc.vector.quantize_mx(
+                out=codes[i][:].rearrange("p g r -> p (g r)").bitcast(FP8X4),
+                scales=scales[i][:].rearrange("p g r -> p (g r)"),
+                in_=grouped[i][:].rearrange("p g r t -> p (g r t)"),
+            )
+
+        def project(i):
+            acc[i] = psum_o.tile([P, N_PAD], F32, name="acc")
+            for g in range(PASSES):
+                nc.tensor.matmul_mx(
+                    out=acc[i][:],
+                    lhsT=codes[i][:, g, :].bitcast(FP8X4),
+                    lhsT_scale=scales[i][:, g, :],
+                    rhs=w_codes[:, g, :].bitcast(FP8X4),
+                    rhs_scale=w_scales[:, g, :],
+                    start=(g == 0),
+                    stop=(g == PASSES - 1),
+                )
+
+        def copy_out(i):
+            c, j = divmod(i, CHUNK)
+            if j == 0:
+                out_tiles[c] = out_pool.tile([P, 3 * HEADS, CHUNK, DH], F32, name="out_chunk")
+            nc.scalar.copy(
+                out=out_tiles[c][:, :, j, :],
+                in_=acc[i][:, 0:C].rearrange("p (a d) -> p a d", d=DH),
+            )
+
+        def store(c):
+            b, q = divmod(c, CHUNKS_PER_BATCH)
+            for w in range(3):
+                rows = outs[w][b].rearrange("n (p s) d -> p n s d", s=ROWS)
+                nc.sync.dma_start(
+                    out=rows[:, :, q * CHUNK : (q + 1) * CHUNK, :],
+                    in_=out_tiles[c][:, w * HEADS : (w + 1) * HEADS, :, :],
+                )
+
+        def due(step, lag):
+            i = step - lag
+            return i if 0 <= i < TILES else None
+
+        def ends_chunk(i):
+            return i is not None and i % CHUNK == CHUNK - 1
+
+        for step in range(TILES + COPY_OUT_LAG + 1):
+            if step % CHUNK == 0 and step // CHUNK + PREFETCH < CHUNKS:
+                load(step // CHUNK + PREFETCH)
+
+            i = due(step, 0)
+            if i is not None:
+                row_sum(i)
+            if ends_chunk(i):
+                mean(i // CHUNK)
+
+            i = due(step, SQUARES_LAG)
+            if i is not None:
+                squares(i)
+            if ends_chunk(i):
+                deviation(i // CHUNK)
+
+            i = due(step, NORMALISE_LAG)
+            if i is not None:
+                normalise(i)
+
+            i = due(step, TRANSPOSE_LAG)
+            if i is not None:
+                transpose(i)
+
+            i = due(step, GAIN_LAG)
+            if i is not None:
+                gain(i)
+
+            i = due(step, QUANTISE_LAG)
+            if i == 0:
+                quantise_weights()
+            if i is not None:
+                quantise(i)
+
+            i = due(step, RSTD_LAG)
+            if ends_chunk(i):
+                inverse_deviation(i // CHUNK)
+
+            i = due(step, MATMUL_LAG)
+            if i is not None:
+                project(i)
+
+            i = due(step, COPY_OUT_LAG)
+            if i is not None:
+                copy_out(i)
+            if ends_chunk(i):
+                store(i // CHUNK)

@@ -29,14 +29,11 @@ CHUNKS = TILES // CHUNK
 CHUNKS_PER_BATCH = ROWS // CHUNK
 PREFETCH = 2
 
-SQUARES_LAG = 4
-RSTD_LAG = 5
-NORMALISE_LAG = 9
-TRANSPOSE_LAG = 11
-GAIN_LAG = 12
-QUANTISE_LAG = 13
-MATMUL_LAG = 14
-COPY_OUT_LAG = 15
+SQUARES_LAG = 1
+NORMALISE_LAG = 5
+GAIN_LAG = NORMALISE_LAG + 1
+QUANTISE_LAG = GAIN_LAG + 1
+TRANSPOSE_AHEAD = 2
 
 FLOPS = 2 * BATCH * TOKENS * D * C
 
@@ -47,14 +44,14 @@ def tile_traceableencoderlayer_pa_t_kernel(tc, x, ln1_w, qkv_w, out_0, out_1, ou
 
     with ExitStack() as ctx:
         const = ctx.enter_context(tc.tile_pool(name="const", bufs=1))
-        x_pool = ctx.enter_context(tc.tile_pool(name="x_pool", bufs=6))
-        stats = ctx.enter_context(tc.tile_pool(name="stats", bufs=4))
+        x_pool = ctx.enter_context(tc.tile_pool(name="x_pool", bufs=PREFETCH + NORMALISE_LAG + 1))
+        stats = ctx.enter_context(tc.tile_pool(name="stats", bufs=NORMALISE_LAG + 2))
         scrap = ctx.enter_context(tc.tile_pool(name="scrap", bufs=2))
-        y_pool = ctx.enter_context(tc.tile_pool(name="y_pool", bufs=4))
-        mx_pool = ctx.enter_context(tc.tile_pool(name="mx_pool", bufs=3))
+        y_pool = ctx.enter_context(tc.tile_pool(name="y_pool", bufs=2 * CHUNK))
+        mx_pool = ctx.enter_context(tc.tile_pool(name="mx_pool", bufs=2))
         out_pool = ctx.enter_context(tc.tile_pool(name="out_pool", bufs=3))
-        psum_t = ctx.enter_context(tc.psum_pool(name="psum_t", bufs=4))
-        psum_o = ctx.enter_context(tc.psum_pool(name="psum_o", bufs=3))
+        psum_t = ctx.enter_context(tc.psum_pool(name="psum_t", bufs=PASSES * TRANSPOSE_AHEAD))
+        psum_o = ctx.enter_context(tc.psum_pool(name="psum_o", bufs=CHUNK))
         ctx.enter_context(tc.manual_schedule())
 
         x_tiles, sums, neg_mean, sq_sums, rstd = {}, {}, {}, {}, {}
@@ -175,36 +172,42 @@ def tile_traceableencoderlayer_pa_t_kernel(tc, x, ln1_w, qkv_w, out_0, out_1, ou
                 turned[i].append(bank)
 
         def gain(i):
-            grouped[i] = mx_pool.tile([P, PASSES, P, PACK], BF16, name="grouped", align_bytes=64)
+            c, j = divmod(i, CHUNK)
+            if j == 0:
+                grouped[c] = mx_pool.tile(
+                    [P, CHUNK, PASSES, P, PACK], BF16, name="grouped", align_bytes=64
+                )
             for g in range(PASSES):
                 nc.vector.tensor_tensor(
-                    out=grouped[i][:, g, :, :],
+                    out=grouped[c][:, j, g, :, :],
                     in0=turned[i][g][:].rearrange("p t r -> p r t"),
                     in1=gain_cols[:, g * PACK : (g + 1) * PACK].unsqueeze(1).to_broadcast([P, P, PACK]),
                     op=ALU.mult,
                 )
 
-        def quantise(i):
-            codes[i] = mx_pool.tile([P, PASSES, P], U32, name="codes", align_bytes=64)
-            scales[i] = mx_pool.tile([P, PASSES, P], U8, name="scales", align_bytes=64)
+        def quantise(c):
+            codes[c] = mx_pool.tile([P, CHUNK, PASSES, P], U32, name="codes", align_bytes=64)
+            scales[c] = mx_pool.tile([P, CHUNK, PASSES, P], U8, name="scales", align_bytes=64)
             nc.vector.quantize_mx(
-                out=codes[i][:].rearrange("p g r -> p (g r)").bitcast(FP8X4),
-                scales=scales[i][:].rearrange("p g r -> p (g r)"),
-                in_=grouped[i][:].rearrange("p g r t -> p (g r t)"),
+                out=codes[c][:].rearrange("p j g r -> p (j g r)").bitcast(FP8X4),
+                scales=scales[c][:].rearrange("p j g r -> p (j g r)"),
+                in_=grouped[c][:].rearrange("p j g r t -> p (j g r t)"),
             )
 
-        def project(i):
-            acc[i] = psum_o.tile([P, N_PAD], F32, name="acc")
-            for g in range(PASSES):
-                nc.tensor.matmul_mx(
-                    out=acc[i][:],
-                    lhsT=codes[i][:, g, :].bitcast(FP8X4),
-                    lhsT_scale=scales[i][:, g, :],
-                    rhs=w_codes[:, g, :].bitcast(FP8X4),
-                    rhs_scale=w_scales[:, g, :],
-                    start=(g == 0),
-                    stop=(g == PASSES - 1),
-                )
+        def project(c):
+            for j in range(CHUNK):
+                i = c * CHUNK + j
+                acc[i] = psum_o.tile([P, N_PAD], F32, name="acc")
+                for g in range(PASSES):
+                    nc.tensor.matmul_mx(
+                        out=acc[i][:],
+                        lhsT=codes[c][:, j, g, :].bitcast(FP8X4),
+                        lhsT_scale=scales[c][:, j, g, :],
+                        rhs=w_codes[:, g, :].bitcast(FP8X4),
+                        rhs_scale=w_scales[:, g, :],
+                        start=(g == 0),
+                        stop=(g == PASSES - 1),
+                    )
 
         def copy_out(i):
             c, j = divmod(i, CHUNK)
@@ -225,56 +228,47 @@ def tile_traceableencoderlayer_pa_t_kernel(tc, x, ln1_w, qkv_w, out_0, out_1, ou
                 )
 
         def due(step, lag):
-            i = step - lag
-            return i if 0 <= i < TILES else None
+            c = step - lag
+            return c if 0 <= c < CHUNKS else None
 
-        def ends_chunk(i):
-            return i is not None and i % CHUNK == CHUNK - 1
+        for step in range(CHUNKS + QUANTISE_LAG):
+            summed = due(step, 0)
+            squared = due(step, SQUARES_LAG)
+            normalised = due(step, NORMALISE_LAG)
+            gained = due(step, GAIN_LAG)
+            quantised = due(step, QUANTISE_LAG)
 
-        for step in range(TILES + COPY_OUT_LAG + 1):
-            if step % CHUNK == 0 and step // CHUNK + PREFETCH < CHUNKS:
-                load(step // CHUNK + PREFETCH)
+            if due(step, -PREFETCH) is not None:
+                load(step + PREFETCH)
 
-            i = due(step, 0)
-            if i is not None:
-                row_sum(i)
-            if ends_chunk(i):
-                mean(i // CHUNK)
-
-            i = due(step, SQUARES_LAG)
-            if i is not None:
-                squares(i)
-            if ends_chunk(i):
-                deviation(i // CHUNK)
-
-            i = due(step, NORMALISE_LAG)
-            if i is not None:
-                normalise(i)
-
-            i = due(step, TRANSPOSE_LAG)
-            if i is not None:
-                transpose(i)
-
-            i = due(step, GAIN_LAG)
-            if i is not None:
-                gain(i)
-
-            i = due(step, QUANTISE_LAG)
-            if i == 0:
+            if squared is not None:
+                mean(squared)
+            if quantised == 0:
                 quantise_weights()
-            if i is not None:
-                quantise(i)
+            if quantised is not None:
+                quantise(quantised)
+            if normalised is not None:
+                inverse_deviation(normalised)
 
-            i = due(step, RSTD_LAG)
-            if ends_chunk(i):
-                inverse_deviation(i // CHUNK)
+            if quantised is not None:
+                project(quantised)
 
-            i = due(step, MATMUL_LAG)
-            if i is not None:
-                project(i)
+            for j in range(CHUNK):
+                if summed is not None:
+                    row_sum(summed * CHUNK + j)
+                if squared is not None:
+                    squares(squared * CHUNK + j)
+                if normalised is not None:
+                    normalise(normalised * CHUNK + j)
+                if gained is not None:
+                    gain(gained * CHUNK + j)
+                i = (step - GAIN_LAG) * CHUNK + j + TRANSPOSE_AHEAD
+                if 0 <= i < TILES:
+                    transpose(i)
+                if quantised is not None:
+                    copy_out(quantised * CHUNK + j)
 
-            i = due(step, COPY_OUT_LAG)
-            if i is not None:
-                copy_out(i)
-            if ends_chunk(i):
-                store(i // CHUNK)
+            if squared is not None:
+                deviation(squared)
+            if quantised is not None:
+                store(quantised)

@@ -21,15 +21,19 @@ PACK = 4
 K_PASS = P * PACK
 PASSES = D // K_PASS
 N_PAD = 512
+COLUMN_GROUPS = ((0, 256), (256, C))
+BN_WIDTH = 512
+BN_DIM = 6
 
 ROWS = TOKENS // P
 CHUNK = 4
+HALF = CHUNK // 2
 TILES = BATCH * ROWS
 CHUNKS = TILES // CHUNK
 CHUNKS_PER_BATCH = ROWS // CHUNK
 PREFETCH = 2
 
-SQUARES_LAG = 1
+DEVIATION_LAG = 1
 NORMALISE_LAG = 5
 GAIN_LAG = NORMALISE_LAG + 1
 QUANTISE_LAG = GAIN_LAG + 1
@@ -54,7 +58,7 @@ def tile_traceableencoderlayer_pa_t_kernel(tc, x, ln1_w, qkv_w, out_0, out_1, ou
         psum_o = ctx.enter_context(tc.psum_pool(name="psum_o", bufs=CHUNK))
         ctx.enter_context(tc.manual_schedule())
 
-        x_tiles, sums, neg_mean, sq_sums, rstd = {}, {}, {}, {}, {}
+        x_tiles, bn_parts, mean_var, sums, neg_mean, sq_sums, std, rstd = {}, {}, {}, {}, {}, {}, {}, {}
         y_tiles, turned, grouped, codes, scales, acc, out_tiles = {}, {}, {}, {}, {}, {}, {}
 
         def load(c):
@@ -105,49 +109,66 @@ def tile_traceableencoderlayer_pa_t_kernel(tc, x, ln1_w, qkv_w, out_0, out_1, ou
                 in_=w_grouped[:].rearrange("p g c t -> p (g c t)"),
             )
 
-        def row_sum(i):
+        def vector_statistics(i):
             c, j = divmod(i, CHUNK)
             if j == 0:
-                sums[c] = stats.tile([P, CHUNK], F32, name="sums")
-            unread = scrap.tile([P, D], BF16, name="unread_v")
-            nc.vector.tensor_scalar(
+                bn_parts[c] = stats.tile([P, HALF, D // BN_WIDTH, BN_DIM], F32, name="bn_parts")
+            for h in range(D // BN_WIDTH):
+                nc.vector.bn_stats(
+                    out=bn_parts[c][:, j // 2, h, :],
+                    in_=x_tiles[c][:, j, h * BN_WIDTH : (h + 1) * BN_WIDTH],
+                )
+
+        def vector_mean_and_variance(c):
+            mean_var[c] = stats.tile([P, HALF, 2], F32, name="mean_var")
+            for n in range(HALF):
+                nc.vector.bn_aggr(
+                    out=mean_var[c][:, n, :], in_=bn_parts[c][:, n, :, :].rearrange("p h s -> p (h s)")
+                )
+            neg_mean[c, 0] = stats.tile([P, HALF], F32, name="neg_mean_v")
+            nc.vector.tensor_scalar_mul(out=neg_mean[c, 0][:], in0=mean_var[c][:, :, 0], scalar1=-1.0)
+
+        def scalar_sum(i):
+            c, j = divmod(i, CHUNK)
+            if j == 1:
+                sums[c] = stats.tile([P, HALF], F32, name="sums")
+            unread = scrap.tile([P, D], BF16, name="unread")
+            nc.scalar.activation(
                 out=unread[:],
-                in0=x_tiles[c][:, j, :],
-                scalar1=1.0,
-                scalar2=None,
-                op0=ALU.mult,
-                op1=ALU.add,
-                accum_out=sums[c][:, j : j + 1],
+                in_=x_tiles[c][:, j, :],
+                func=ACT.Identity,
+                accum_out=sums[c][:, j // 2 : j // 2 + 1],
             )
 
-        def mean(c):
-            neg_mean[c] = stats.tile([P, CHUNK], F32, name="neg_mean")
-            nc.vector.tensor_scalar_mul(out=neg_mean[c][:], in0=sums[c][:], scalar1=-1.0 / D)
+        def scalar_mean(c):
+            neg_mean[c, 1] = stats.tile([P, HALF], F32, name="neg_mean_s")
+            nc.scalar.mul(out=neg_mean[c, 1][:], in_=sums[c][:], mul=-1.0 / D)
 
-        def squares(i):
+        def scalar_squares(i):
             c, j = divmod(i, CHUNK)
-            if j == 0:
-                sq_sums[c] = stats.tile([P, CHUNK], F32, name="sq_sums")
-            unread = scrap.tile([P, D], BF16, name="unread_s")
+            if j == 1:
+                sq_sums[c] = stats.tile([P, HALF], F32, name="sq_sums")
+            unread = scrap.tile([P, D], BF16, name="unread")
             nc.scalar.activation(
                 out=unread[:],
                 in_=x_tiles[c][:, j, :],
                 func=ACT.Square,
-                bias=neg_mean[c][:, j : j + 1],
+                bias=neg_mean[c, 1][:, j // 2 : j // 2 + 1],
                 scale=1.0,
-                accum_out=sq_sums[c][:, j : j + 1],
+                accum_out=sq_sums[c][:, j // 2 : j // 2 + 1],
             )
 
-        std = {}
-
         def deviation(c):
-            std[c] = stats.tile([P, CHUNK], F32, name="std")
+            std[c] = stats.tile([P, 2, HALF], F32, name="std")
             nc.scalar.activation(
-                out=std[c][:], in_=sq_sums[c][:], func=ACT.Sqrt, bias=eps[:, 0:1], scale=1.0 / D
+                out=std[c][:, 0, :], in_=mean_var[c][:, :, 1], func=ACT.Sqrt, bias=eps[:, 0:1], scale=1.0
+            )
+            nc.scalar.activation(
+                out=std[c][:, 1, :], in_=sq_sums[c][:], func=ACT.Sqrt, bias=eps[:, 0:1], scale=1.0 / D
             )
 
         def inverse_deviation(c):
-            rstd[c] = stats.tile([P, CHUNK], F32, name="rstd")
+            rstd[c] = stats.tile([P, 2, HALF], F32, name="rstd")
             nc.vector.reciprocal(out=rstd[c][:], in_=std[c][:])
 
         def normalise(i):
@@ -156,8 +177,8 @@ def tile_traceableencoderlayer_pa_t_kernel(tc, x, ln1_w, qkv_w, out_0, out_1, ou
             nc.gpsimd.tensor_scalar(
                 out=y_tiles[i][:],
                 in0=x_tiles[c][:, j, :],
-                scalar1=neg_mean[c][:, j : j + 1],
-                scalar2=rstd[c][:, j : j + 1],
+                scalar1=neg_mean[c, j % 2][:, j // 2 : j // 2 + 1],
+                scalar2=rstd[c][:, j % 2, j // 2 : j // 2 + 1],
                 op0=ALU.add,
                 op1=ALU.mult,
             )
@@ -197,17 +218,18 @@ def tile_traceableencoderlayer_pa_t_kernel(tc, x, ln1_w, qkv_w, out_0, out_1, ou
         def project(c):
             for j in range(CHUNK):
                 i = c * CHUNK + j
-                acc[i] = psum_o.tile([P, N_PAD], F32, name="acc")
-                for g in range(PASSES):
-                    nc.tensor.matmul_mx(
-                        out=acc[i][:],
-                        lhsT=codes[c][:, j, g, :].bitcast(FP8X4),
-                        lhsT_scale=scales[c][:, j, g, :],
-                        rhs=w_codes[:, g, :].bitcast(FP8X4),
-                        rhs_scale=w_scales[:, g, :],
-                        start=(g == 0),
-                        stop=(g == PASSES - 1),
-                    )
+                acc[i] = psum_o.tile([P, C], F32, name="acc")
+                for lo, hi in COLUMN_GROUPS:
+                    for g in range(PASSES):
+                        nc.tensor.matmul_mx(
+                            out=acc[i][:, lo:hi],
+                            lhsT=codes[c][:, j, g, :].bitcast(FP8X4),
+                            lhsT_scale=scales[c][:, j, g, :],
+                            rhs=w_codes[:, g, lo:hi].bitcast(FP8X4),
+                            rhs_scale=w_scales[:, g, lo:hi],
+                            start=(g == 0),
+                            stop=(g == PASSES - 1),
+                        )
 
         def copy_out(i):
             c, j = divmod(i, CHUNK)
@@ -215,7 +237,7 @@ def tile_traceableencoderlayer_pa_t_kernel(tc, x, ln1_w, qkv_w, out_0, out_1, ou
                 out_tiles[c] = out_pool.tile([P, 3 * HEADS, CHUNK, DH], F32, name="out_chunk")
             nc.scalar.copy(
                 out=out_tiles[c][:, :, j, :],
-                in_=acc[i][:, 0:C].rearrange("p (a d) -> p a d", d=DH),
+                in_=acc[i][:].rearrange("p (a d) -> p a d", d=DH),
             )
 
         def store(c):
@@ -232,8 +254,8 @@ def tile_traceableencoderlayer_pa_t_kernel(tc, x, ln1_w, qkv_w, out_0, out_1, ou
             return c if 0 <= c < CHUNKS else None
 
         for step in range(CHUNKS + QUANTISE_LAG):
-            summed = due(step, 0)
-            squared = due(step, SQUARES_LAG)
+            measured = due(step, 0)
+            finished = due(step, DEVIATION_LAG)
             normalised = due(step, NORMALISE_LAG)
             gained = due(step, GAIN_LAG)
             quantised = due(step, QUANTISE_LAG)
@@ -241,8 +263,9 @@ def tile_traceableencoderlayer_pa_t_kernel(tc, x, ln1_w, qkv_w, out_0, out_1, ou
             if due(step, -PREFETCH) is not None:
                 load(step + PREFETCH)
 
-            if squared is not None:
-                mean(squared)
+            if finished is not None:
+                vector_mean_and_variance(finished)
+                deviation(finished)
             if quantised == 0:
                 quantise_weights()
             if quantised is not None:
@@ -254,10 +277,10 @@ def tile_traceableencoderlayer_pa_t_kernel(tc, x, ln1_w, qkv_w, out_0, out_1, ou
                 project(quantised)
 
             for j in range(CHUNK):
-                if summed is not None:
-                    row_sum(summed * CHUNK + j)
-                if squared is not None:
-                    squares(squared * CHUNK + j)
+                if measured is not None and j % 2 == 0:
+                    vector_statistics(measured * CHUNK + j)
+                if measured is not None and j % 2 == 1:
+                    scalar_sum(measured * CHUNK + j)
                 if normalised is not None:
                     normalise(normalised * CHUNK + j)
                 if gained is not None:
@@ -268,7 +291,9 @@ def tile_traceableencoderlayer_pa_t_kernel(tc, x, ln1_w, qkv_w, out_0, out_1, ou
                 if quantised is not None:
                     copy_out(quantised * CHUNK + j)
 
-            if squared is not None:
-                deviation(squared)
+            if measured is not None:
+                scalar_mean(measured)
+                for j in range(1, CHUNK, 2):
+                    scalar_squares(measured * CHUNK + j)
             if quantised is not None:
                 store(quantised)

@@ -22,18 +22,16 @@ K_PASS = P * PACK
 PASSES = D // K_PASS
 N_PAD = 512
 COLUMN_GROUPS = ((0, 256), (256, C))
-BN_WIDTH = 512
-BN_DIM = 6
 
 ROWS = TOKENS // P
 CHUNK = 4
-HALF = CHUNK // 2
+GPSIMD_TILES = 3
 TILES = BATCH * ROWS
 CHUNKS = TILES // CHUNK
 CHUNKS_PER_BATCH = ROWS // CHUNK
 PREFETCH = 2
 
-DEVIATION_LAG = 1
+SQUARES_LAG = 1
 NORMALISE_LAG = 5
 GAIN_LAG = NORMALISE_LAG + 1
 QUANTISE_LAG = GAIN_LAG + 1
@@ -58,7 +56,7 @@ def tile_traceableencoderlayer_pa_t_kernel(tc, x, ln1_w, qkv_w, out_0, out_1, ou
         psum_o = ctx.enter_context(tc.psum_pool(name="psum_o", bufs=CHUNK))
         ctx.enter_context(tc.manual_schedule())
 
-        x_tiles, bn_parts, mean_var, sums, neg_mean, sq_sums, std, rstd = {}, {}, {}, {}, {}, {}, {}, {}
+        x_tiles, sums, neg_mean, sq_sums, rstd, shift = {}, {}, {}, {}, {}, {}
         y_tiles, turned, grouped, codes, scales, acc, out_tiles = {}, {}, {}, {}, {}, {}, {}
 
         def load(c):
@@ -109,79 +107,73 @@ def tile_traceableencoderlayer_pa_t_kernel(tc, x, ln1_w, qkv_w, out_0, out_1, ou
                 in_=w_grouped[:].rearrange("p g c t -> p (g c t)"),
             )
 
-        def vector_statistics(i):
+        def row_sum(i):
             c, j = divmod(i, CHUNK)
             if j == 0:
-                bn_parts[c] = stats.tile([P, HALF, D // BN_WIDTH, BN_DIM], F32, name="bn_parts")
-            for h in range(D // BN_WIDTH):
-                nc.vector.bn_stats(
-                    out=bn_parts[c][:, j // 2, h, :],
-                    in_=x_tiles[c][:, j, h * BN_WIDTH : (h + 1) * BN_WIDTH],
-                )
-
-        def vector_mean_and_variance(c):
-            mean_var[c] = stats.tile([P, HALF, 2], F32, name="mean_var")
-            for n in range(HALF):
-                nc.vector.bn_aggr(
-                    out=mean_var[c][:, n, :], in_=bn_parts[c][:, n, :, :].rearrange("p h s -> p (h s)")
-                )
-            neg_mean[c, 0] = stats.tile([P, HALF], F32, name="neg_mean_v")
-            nc.vector.tensor_scalar_mul(out=neg_mean[c, 0][:], in0=mean_var[c][:, :, 0], scalar1=-1.0)
-
-        def scalar_sum(i):
-            c, j = divmod(i, CHUNK)
-            if j == 1:
-                sums[c] = stats.tile([P, HALF], F32, name="sums")
-            unread = scrap.tile([P, D], BF16, name="unread")
-            nc.scalar.activation(
+                sums[c] = stats.tile([P, CHUNK], F32, name="sums")
+            unread = scrap.tile([P, D], BF16, name="unread_v")
+            nc.vector.tensor_scalar(
                 out=unread[:],
-                in_=x_tiles[c][:, j, :],
-                func=ACT.Identity,
-                accum_out=sums[c][:, j // 2 : j // 2 + 1],
+                in0=x_tiles[c][:, j, :],
+                scalar1=1.0,
+                scalar2=None,
+                op0=ALU.mult,
+                op1=ALU.add,
+                accum_out=sums[c][:, j : j + 1],
             )
 
-        def scalar_mean(c):
-            neg_mean[c, 1] = stats.tile([P, HALF], F32, name="neg_mean_s")
-            nc.scalar.mul(out=neg_mean[c, 1][:], in_=sums[c][:], mul=-1.0 / D)
+        def mean(c):
+            neg_mean[c] = stats.tile([P, CHUNK], F32, name="neg_mean")
+            nc.vector.tensor_scalar_mul(out=neg_mean[c][:], in0=sums[c][:], scalar1=-1.0 / D)
 
-        def scalar_squares(i):
+        def squares(i):
             c, j = divmod(i, CHUNK)
-            if j == 1:
-                sq_sums[c] = stats.tile([P, HALF], F32, name="sq_sums")
-            unread = scrap.tile([P, D], BF16, name="unread")
+            if j == 0:
+                sq_sums[c] = stats.tile([P, CHUNK], F32, name="sq_sums")
+            unread = scrap.tile([P, D], BF16, name="unread_s")
             nc.scalar.activation(
                 out=unread[:],
                 in_=x_tiles[c][:, j, :],
                 func=ACT.Square,
-                bias=neg_mean[c, 1][:, j // 2 : j // 2 + 1],
+                bias=neg_mean[c][:, j : j + 1],
                 scale=1.0,
-                accum_out=sq_sums[c][:, j // 2 : j // 2 + 1],
+                accum_out=sq_sums[c][:, j : j + 1],
             )
+
+        std = {}
 
         def deviation(c):
-            std[c] = stats.tile([P, 2, HALF], F32, name="std")
+            std[c] = stats.tile([P, CHUNK], F32, name="std")
             nc.scalar.activation(
-                out=std[c][:, 0, :], in_=mean_var[c][:, :, 1], func=ACT.Sqrt, bias=eps[:, 0:1], scale=1.0
-            )
-            nc.scalar.activation(
-                out=std[c][:, 1, :], in_=sq_sums[c][:], func=ACT.Sqrt, bias=eps[:, 0:1], scale=1.0 / D
+                out=std[c][:], in_=sq_sums[c][:], func=ACT.Sqrt, bias=eps[:, 0:1], scale=1.0 / D
             )
 
-        def inverse_deviation(c):
-            rstd[c] = stats.tile([P, 2, HALF], F32, name="rstd")
+        def scale_and_shift(c):
+            rstd[c] = stats.tile([P, CHUNK], F32, name="rstd")
             nc.vector.reciprocal(out=rstd[c][:], in_=std[c][:])
+            shift[c] = stats.tile([P, CHUNK], F32, name="shift")
+            nc.vector.tensor_tensor(out=shift[c][:], in0=neg_mean[c][:], in1=rstd[c][:], op=ALU.mult)
 
         def normalise(i):
             c, j = divmod(i, CHUNK)
             y_tiles[i] = y_pool.tile([P, D], F32, name="y")
-            nc.gpsimd.tensor_scalar(
-                out=y_tiles[i][:],
-                in0=x_tiles[c][:, j, :],
-                scalar1=neg_mean[c, j % 2][:, j // 2 : j // 2 + 1],
-                scalar2=rstd[c][:, j % 2, j // 2 : j // 2 + 1],
-                op0=ALU.add,
-                op1=ALU.mult,
-            )
+            if j < GPSIMD_TILES:
+                nc.gpsimd.tensor_scalar(
+                    out=y_tiles[i][:],
+                    in0=x_tiles[c][:, j, :],
+                    scalar1=rstd[c][:, j : j + 1],
+                    scalar2=shift[c][:, j : j + 1],
+                    op0=ALU.mult,
+                    op1=ALU.add,
+                )
+            else:
+                nc.scalar.activation(
+                    out=y_tiles[i][:],
+                    in_=x_tiles[c][:, j, :],
+                    func=ACT.Identity,
+                    bias=shift[c][:, j : j + 1],
+                    scale=rstd[c][:, j : j + 1],
+                )
 
         def transpose(i):
             turned[i] = []
@@ -254,8 +246,8 @@ def tile_traceableencoderlayer_pa_t_kernel(tc, x, ln1_w, qkv_w, out_0, out_1, ou
             return c if 0 <= c < CHUNKS else None
 
         for step in range(CHUNKS + QUANTISE_LAG):
-            measured = due(step, 0)
-            finished = due(step, DEVIATION_LAG)
+            summed = due(step, 0)
+            squared = due(step, SQUARES_LAG)
             normalised = due(step, NORMALISE_LAG)
             gained = due(step, GAIN_LAG)
             quantised = due(step, QUANTISE_LAG)
@@ -263,24 +255,23 @@ def tile_traceableencoderlayer_pa_t_kernel(tc, x, ln1_w, qkv_w, out_0, out_1, ou
             if due(step, -PREFETCH) is not None:
                 load(step + PREFETCH)
 
-            if finished is not None:
-                vector_mean_and_variance(finished)
-                deviation(finished)
+            if squared is not None:
+                mean(squared)
             if quantised == 0:
                 quantise_weights()
             if quantised is not None:
                 quantise(quantised)
             if normalised is not None:
-                inverse_deviation(normalised)
+                scale_and_shift(normalised)
 
             if quantised is not None:
                 project(quantised)
 
             for j in range(CHUNK):
-                if measured is not None and j % 2 == 0:
-                    vector_statistics(measured * CHUNK + j)
-                if measured is not None and j % 2 == 1:
-                    scalar_sum(measured * CHUNK + j)
+                if summed is not None:
+                    row_sum(summed * CHUNK + j)
+                if squared is not None:
+                    squares(squared * CHUNK + j)
                 if normalised is not None:
                     normalise(normalised * CHUNK + j)
                 if gained is not None:
@@ -291,9 +282,7 @@ def tile_traceableencoderlayer_pa_t_kernel(tc, x, ln1_w, qkv_w, out_0, out_1, ou
                 if quantised is not None:
                     copy_out(quantised * CHUNK + j)
 
-            if measured is not None:
-                scalar_mean(measured)
-                for j in range(1, CHUNK, 2):
-                    scalar_squares(measured * CHUNK + j)
+            if squared is not None:
+                deviation(squared)
             if quantised is not None:
                 store(quantised)

@@ -21,11 +21,10 @@ PACK = 4
 K_PASS = P * PACK
 PASSES = D // K_PASS
 N_PAD = 512
-COLUMN_GROUPS = ((0, 256), (256, C))
+RUN = 4
 
 ROWS = TOKENS // P
 CHUNK = 4
-GPSIMD_TILES = 3
 TILES = BATCH * ROWS
 CHUNKS = TILES // CHUNK
 CHUNKS_PER_BATCH = ROWS // CHUNK
@@ -56,7 +55,7 @@ def tile_traceableencoderlayer_pa_t_kernel(tc, x, ln1_w, qkv_w, out_0, out_1, ou
         psum_o = ctx.enter_context(tc.psum_pool(name="psum_o", bufs=CHUNK))
         ctx.enter_context(tc.manual_schedule())
 
-        x_tiles, sums, neg_mean, sq_sums, rstd, shift = {}, {}, {}, {}, {}, {}
+        x_tiles, sums, neg_mean, sq_sums, rstd = {}, {}, {}, {}, {}
         y_tiles, turned, grouped, codes, scales, acc, out_tiles = {}, {}, {}, {}, {}, {}, {}
 
         def load(c):
@@ -148,32 +147,21 @@ def tile_traceableencoderlayer_pa_t_kernel(tc, x, ln1_w, qkv_w, out_0, out_1, ou
                 out=std[c][:], in_=sq_sums[c][:], func=ACT.Sqrt, bias=eps[:, 0:1], scale=1.0 / D
             )
 
-        def scale_and_shift(c):
+        def inverse_deviation(c):
             rstd[c] = stats.tile([P, CHUNK], F32, name="rstd")
             nc.vector.reciprocal(out=rstd[c][:], in_=std[c][:])
-            shift[c] = stats.tile([P, CHUNK], F32, name="shift")
-            nc.vector.tensor_tensor(out=shift[c][:], in0=neg_mean[c][:], in1=rstd[c][:], op=ALU.mult)
 
         def normalise(i):
             c, j = divmod(i, CHUNK)
             y_tiles[i] = y_pool.tile([P, D], F32, name="y")
-            if j < GPSIMD_TILES:
-                nc.gpsimd.tensor_scalar(
-                    out=y_tiles[i][:],
-                    in0=x_tiles[c][:, j, :],
-                    scalar1=rstd[c][:, j : j + 1],
-                    scalar2=shift[c][:, j : j + 1],
-                    op0=ALU.mult,
-                    op1=ALU.add,
-                )
-            else:
-                nc.scalar.activation(
-                    out=y_tiles[i][:],
-                    in_=x_tiles[c][:, j, :],
-                    func=ACT.Identity,
-                    bias=shift[c][:, j : j + 1],
-                    scale=rstd[c][:, j : j + 1],
-                )
+            nc.gpsimd.tensor_scalar(
+                out=y_tiles[i][:],
+                in0=x_tiles[c][:, j, :],
+                scalar1=neg_mean[c][:, j : j + 1],
+                scalar2=rstd[c][:, j : j + 1],
+                op0=ALU.add,
+                op1=ALU.mult,
+            )
 
         def transpose(i):
             turned[i] = []
@@ -191,10 +179,11 @@ def tile_traceableencoderlayer_pa_t_kernel(tc, x, ln1_w, qkv_w, out_0, out_1, ou
                     [P, CHUNK, PASSES, P, PACK], BF16, name="grouped", align_bytes=64
                 )
             for g in range(PASSES):
+                gains = gain_cols[:, g * PACK : (g + 1) * PACK].unsqueeze(1).unsqueeze(3)
                 nc.vector.tensor_tensor(
-                    out=grouped[c][:, j, g, :, :],
-                    in0=turned[i][g][:].rearrange("p t r -> p r t"),
-                    in1=gain_cols[:, g * PACK : (g + 1) * PACK].unsqueeze(1).to_broadcast([P, P, PACK]),
+                    out=grouped[c][:, j, g, :, :].rearrange("p (n i) t -> p n t i", i=RUN),
+                    in0=turned[i][g][:].rearrange("p t (n i) -> p n t i", i=RUN),
+                    in1=gains.to_broadcast([P, P // RUN, PACK, RUN]),
                     op=ALU.mult,
                 )
 
@@ -210,18 +199,17 @@ def tile_traceableencoderlayer_pa_t_kernel(tc, x, ln1_w, qkv_w, out_0, out_1, ou
         def project(c):
             for j in range(CHUNK):
                 i = c * CHUNK + j
-                acc[i] = psum_o.tile([P, C], F32, name="acc")
-                for lo, hi in COLUMN_GROUPS:
-                    for g in range(PASSES):
-                        nc.tensor.matmul_mx(
-                            out=acc[i][:, lo:hi],
-                            lhsT=codes[c][:, j, g, :].bitcast(FP8X4),
-                            lhsT_scale=scales[c][:, j, g, :],
-                            rhs=w_codes[:, g, lo:hi].bitcast(FP8X4),
-                            rhs_scale=w_scales[:, g, lo:hi],
-                            start=(g == 0),
-                            stop=(g == PASSES - 1),
-                        )
+                acc[i] = psum_o.tile([P, N_PAD], F32, name="acc")
+                for g in range(PASSES):
+                    nc.tensor.matmul_mx(
+                        out=acc[i][:],
+                        lhsT=codes[c][:, j, g, :].bitcast(FP8X4),
+                        lhsT_scale=scales[c][:, j, g, :],
+                        rhs=w_codes[:, g, :].bitcast(FP8X4),
+                        rhs_scale=w_scales[:, g, :],
+                        start=(g == 0),
+                        stop=(g == PASSES - 1),
+                    )
 
         def copy_out(i):
             c, j = divmod(i, CHUNK)
@@ -229,7 +217,7 @@ def tile_traceableencoderlayer_pa_t_kernel(tc, x, ln1_w, qkv_w, out_0, out_1, ou
                 out_tiles[c] = out_pool.tile([P, 3 * HEADS, CHUNK, DH], F32, name="out_chunk")
             nc.scalar.copy(
                 out=out_tiles[c][:, :, j, :],
-                in_=acc[i][:].rearrange("p (a d) -> p a d", d=DH),
+                in_=acc[i][:, 0:C].rearrange("p (a d) -> p a d", d=DH),
             )
 
         def store(c):
@@ -262,7 +250,7 @@ def tile_traceableencoderlayer_pa_t_kernel(tc, x, ln1_w, qkv_w, out_0, out_1, ou
             if quantised is not None:
                 quantise(quantised)
             if normalised is not None:
-                scale_and_shift(normalised)
+                inverse_deviation(normalised)
 
             if quantised is not None:
                 project(quantised)

@@ -21,10 +21,10 @@ PACK = 4
 K_PASS = P * PACK
 PASSES = D // K_PASS
 N_PAD = 512
-RUN = 4
 
 ROWS = TOKENS // P
 CHUNK = 4
+VECTOR_SUMS = 3
 TILES = BATCH * ROWS
 CHUNKS = TILES // CHUNK
 CHUNKS_PER_BATCH = ROWS // CHUNK
@@ -55,7 +55,7 @@ def tile_traceableencoderlayer_pa_t_kernel(tc, x, ln1_w, qkv_w, out_0, out_1, ou
         psum_o = ctx.enter_context(tc.psum_pool(name="psum_o", bufs=CHUNK))
         ctx.enter_context(tc.manual_schedule())
 
-        x_tiles, sums, neg_mean, sq_sums, rstd = {}, {}, {}, {}, {}
+        x_tiles, sums, sums_s, neg_mean, sq_sums, rstd = {}, {}, {}, {}, {}, {}
         y_tiles, turned, grouped, codes, scales, acc, out_tiles = {}, {}, {}, {}, {}, {}, {}
 
         def load(c):
@@ -109,21 +109,40 @@ def tile_traceableencoderlayer_pa_t_kernel(tc, x, ln1_w, qkv_w, out_0, out_1, ou
         def row_sum(i):
             c, j = divmod(i, CHUNK)
             if j == 0:
-                sums[c] = stats.tile([P, CHUNK], F32, name="sums")
-            unread = scrap.tile([P, D], BF16, name="unread_v")
-            nc.vector.tensor_scalar(
-                out=unread[:],
-                in0=x_tiles[c][:, j, :],
-                scalar1=1.0,
-                scalar2=None,
-                op0=ALU.mult,
-                op1=ALU.add,
-                accum_out=sums[c][:, j : j + 1],
-            )
+                sums[c] = stats.tile([P, VECTOR_SUMS], F32, name="sums_v")
+            if j == VECTOR_SUMS:
+                sums_s[c] = stats.tile([P, CHUNK - VECTOR_SUMS], F32, name="sums_s")
+            if j < VECTOR_SUMS:
+                unread = scrap.tile([P, D], BF16, name="unread_v")
+                nc.vector.tensor_scalar(
+                    out=unread[:],
+                    in0=x_tiles[c][:, j, :],
+                    scalar1=1.0,
+                    scalar2=None,
+                    op0=ALU.mult,
+                    op1=ALU.add,
+                    accum_out=sums[c][:, j : j + 1],
+                )
+            else:
+                unread = scrap.tile([P, D], BF16, name="unread_s")
+                nc.scalar.activation(
+                    out=unread[:],
+                    in_=x_tiles[c][:, j, :],
+                    func=ACT.Identity,
+                    accum_out=sums_s[c][:, j - VECTOR_SUMS : j - VECTOR_SUMS + 1],
+                )
 
-        def mean(c):
-            neg_mean[c] = stats.tile([P, CHUNK], F32, name="neg_mean")
-            nc.vector.tensor_scalar_mul(out=neg_mean[c][:], in0=sums[c][:], scalar1=-1.0 / D)
+        def vector_mean(c):
+            means = stats.tile([P, VECTOR_SUMS], F32, name="neg_mean_v")
+            nc.vector.tensor_scalar_mul(out=means[:], in0=sums[c][:], scalar1=-1.0 / D)
+            for j in range(VECTOR_SUMS):
+                neg_mean[c * CHUNK + j] = means[:, j : j + 1]
+
+        def scalar_mean(c):
+            means = stats.tile([P, CHUNK - VECTOR_SUMS], F32, name="neg_mean_s")
+            nc.scalar.mul(out=means[:], in_=sums_s[c][:], mul=-1.0 / D)
+            for j in range(VECTOR_SUMS, CHUNK):
+                neg_mean[c * CHUNK + j] = means[:, j - VECTOR_SUMS : j - VECTOR_SUMS + 1]
 
         def squares(i):
             c, j = divmod(i, CHUNK)
@@ -134,7 +153,7 @@ def tile_traceableencoderlayer_pa_t_kernel(tc, x, ln1_w, qkv_w, out_0, out_1, ou
                 out=unread[:],
                 in_=x_tiles[c][:, j, :],
                 func=ACT.Square,
-                bias=neg_mean[c][:, j : j + 1],
+                bias=neg_mean[i],
                 scale=1.0,
                 accum_out=sq_sums[c][:, j : j + 1],
             )
@@ -157,7 +176,7 @@ def tile_traceableencoderlayer_pa_t_kernel(tc, x, ln1_w, qkv_w, out_0, out_1, ou
             nc.gpsimd.tensor_scalar(
                 out=y_tiles[i][:],
                 in0=x_tiles[c][:, j, :],
-                scalar1=neg_mean[c][:, j : j + 1],
+                scalar1=neg_mean[i],
                 scalar2=rstd[c][:, j : j + 1],
                 op0=ALU.add,
                 op1=ALU.mult,
@@ -179,11 +198,10 @@ def tile_traceableencoderlayer_pa_t_kernel(tc, x, ln1_w, qkv_w, out_0, out_1, ou
                     [P, CHUNK, PASSES, P, PACK], BF16, name="grouped", align_bytes=64
                 )
             for g in range(PASSES):
-                gains = gain_cols[:, g * PACK : (g + 1) * PACK].unsqueeze(1).unsqueeze(3)
                 nc.vector.tensor_tensor(
-                    out=grouped[c][:, j, g, :, :].rearrange("p (n i) t -> p n t i", i=RUN),
-                    in0=turned[i][g][:].rearrange("p t (n i) -> p n t i", i=RUN),
-                    in1=gains.to_broadcast([P, P // RUN, PACK, RUN]),
+                    out=grouped[c][:, j, g, :, :],
+                    in0=turned[i][g][:].rearrange("p t r -> p r t"),
+                    in1=gain_cols[:, g * PACK : (g + 1) * PACK].unsqueeze(1).to_broadcast([P, P, PACK]),
                     op=ALU.mult,
                 )
 
@@ -244,7 +262,7 @@ def tile_traceableencoderlayer_pa_t_kernel(tc, x, ln1_w, qkv_w, out_0, out_1, ou
                 load(step + PREFETCH)
 
             if squared is not None:
-                mean(squared)
+                vector_mean(squared)
             if quantised == 0:
                 quantise_weights()
             if quantised is not None:
@@ -270,6 +288,8 @@ def tile_traceableencoderlayer_pa_t_kernel(tc, x, ln1_w, qkv_w, out_0, out_1, ou
                 if quantised is not None:
                     copy_out(quantised * CHUNK + j)
 
+            if summed is not None:
+                scalar_mean(summed)
             if squared is not None:
                 deviation(squared)
             if quantised is not None:

from contextlib import ExitStack

import concourse.mybir as mybir
from concourse.masks import make_identity

BF16 = mybir.dt.bfloat16
F32 = mybir.dt.float32
U32 = mybir.dt.uint32
U8 = mybir.dt.uint8
FP8X4 = mybir.dt.float8_e4m3fn_x4
ALU = mybir.AluOpType
ACT = mybir.ActivationFunctionType

BATCH, TOKENS, D = 4, 2048, 1024
HEADS, DH = 4, 32
C = 3 * HEADS * DH
EPS = 1e-5

P = 128
PACK = 4
K_PASS = P * PACK
PASSES = D // K_PASS
N_PAD = 512

ROWS = TOKENS // P
CHUNK = 4
VECTOR_SUMS = 3
TILES = BATCH * ROWS
CHUNKS = TILES // CHUNK
CHUNKS_PER_BATCH = ROWS // CHUNK
PREFETCH = 2

SQUARES_LAG = 1
NORMALISE_LAG = 5
GAIN_LAG = NORMALISE_LAG + 1
QUANTISE_LAG = GAIN_LAG + 1
TRANSPOSE_AHEAD = 2

FLOPS = 2 * BATCH * TOKENS * D * C


def tile_traceableencoderlayer_pa_t_kernel(tc, x, ln1_w, qkv_w, out_0, out_1, out_2):
    nc = tc.nc
    outs = (out_0, out_1, out_2)

    with ExitStack() as ctx:
        const = ctx.enter_context(tc.tile_pool(name="const", bufs=1))
        x_pool = ctx.enter_context(tc.tile_pool(name="x_pool", bufs=PREFETCH + NORMALISE_LAG + 1))
        stats = ctx.enter_context(tc.tile_pool(name="stats", bufs=NORMALISE_LAG + 2))
        scrap = ctx.enter_context(tc.tile_pool(name="scrap", bufs=2))
        y_pool = ctx.enter_context(tc.tile_pool(name="y_pool", bufs=2 * CHUNK))
        mx_pool = ctx.enter_context(tc.tile_pool(name="mx_pool", bufs=2))
        out_pool = ctx.enter_context(tc.tile_pool(name="out_pool", bufs=3))
        psum_t = ctx.enter_context(tc.psum_pool(name="psum_t", bufs=PASSES * TRANSPOSE_AHEAD))
        psum_o = ctx.enter_context(tc.psum_pool(name="psum_o", bufs=CHUNK))
        ctx.enter_context(tc.manual_schedule())

        x_tiles, sums, sums_s, neg_mean, sq_sums, rstd = {}, {}, {}, {}, {}, {}
        y_tiles, turned, grouped, codes, scales, acc, out_tiles = {}, {}, {}, {}, {}, {}, {}

        def load(c):
            b, q = divmod(c, CHUNKS_PER_BATCH)
            x_tiles[c] = x_pool.tile([P, CHUNK, D], BF16, name="x_chunk")
            rows = x[b].rearrange("(p s) k -> p s k", s=ROWS)
            nc.sync.dma_start(out=x_tiles[c][:], in_=rows[:, q * CHUNK : (q + 1) * CHUNK, :])

        w_raw = const.tile([P, C // P, D], BF16, name="w_raw")
        nc.sync.dma_start(out=w_raw[:], in_=qkv_w.rearrange("(a p) k -> p a k", p=P))
        gain_rows = const.tile([P, P], BF16, name="gain_rows")
        nc.vector.memset(gain_rows[:], 0.0)
        nc.sync.dma_start(out=gain_rows[0 : D // P, :], in_=ln1_w.rearrange("(j p) -> j p", p=P))
        for c in range(PREFETCH):
            load(c)

        ident_bf = const.tile([P, P], BF16, name="ident_bf")
        make_identity(nc, ident_bf[:])
        ident_f32 = const.tile([P, P], F32, name="ident_f32")
        make_identity(nc, ident_f32[:])
        eps = const.tile([P, 1], F32, name="eps")
        nc.vector.memset(eps[:], EPS)

        w_grouped = const.tile([P, PASSES, N_PAD, PACK], BF16, name="w_grouped", align_bytes=64)
        nc.vector.memset(w_grouped[:], 0.0)
        w_codes = const.tile([P, PASSES, N_PAD], U32, name="w_codes", align_bytes=64)
        w_scales = const.tile([P, PASSES, N_PAD], U8, name="w_scales", align_bytes=64)
        gain_cols = const.tile([P, D // P], F32, name="gain_cols")

        for a in range(C // P):
            w_turned = psum_t.tile([P, PASSES, PACK, P], BF16, name="w_turned", tag="turned")
            for g in range(PASSES):
                for t in range(PACK):
                    k0 = g * K_PASS + t * P
                    nc.tensor.transpose(w_turned[:, g, t, :], w_raw[:, a, k0 : k0 + P], ident_bf[:])
            nc.scalar.copy(
                out=w_grouped[:, :, a * P : (a + 1) * P, :],
                in_=w_turned[:].rearrange("p g t c -> p g c t"),
            )
        gain_turned = psum_t.tile([P, P], BF16, name="gain_turned", tag="turned")
        nc.tensor.transpose(gain_turned[:], gain_rows[:], ident_bf[:])
        nc.scalar.copy(out=gain_cols[:], in_=gain_turned[:, 0 : D // P])

        def quantise_weights():
            nc.vector.quantize_mx(
                out=w_codes[:].rearrange("p g c -> p (g c)").bitcast(FP8X4),
                scales=w_scales[:].rearrange("p g c -> p (g c)"),
                in_=w_grouped[:].rearrange("p g c t -> p (g c t)"),
            )

        def row_sum(i):
            c, j = divmod(i, CHUNK)
            if j == 0:
                sums[c] = stats.tile([P, VECTOR_SUMS], F32, name="sums_v")
            if j == VECTOR_SUMS:
                sums_s[c] = stats.tile([P, CHUNK - VECTOR_SUMS], F32, name="sums_s")
            if j < VECTOR_SUMS:
                unread = scrap.tile([P, D], BF16, name="unread_v")
                nc.vector.tensor_scalar(
                    out=unread[:],
                    in0=x_tiles[c][:, j, :],
                    scalar1=1.0,
                    scalar2=None,
                    op0=ALU.mult,
                    op1=ALU.add,
                    accum_out=sums[c][:, j : j + 1],
                )
            else:
                unread = scrap.tile([P, D], BF16, name="unread_s")
                nc.scalar.activation(
                    out=unread[:],
                    in_=x_tiles[c][:, j, :],
                    func=ACT.Identity,
                    accum_out=sums_s[c][:, j - VECTOR_SUMS : j - VECTOR_SUMS + 1],
                )

        def vector_mean(c):
            means = stats.tile([P, VECTOR_SUMS], F32, name="neg_mean_v")
            nc.vector.tensor_scalar_mul(out=means[:], in0=sums[c][:], scalar1=-1.0 / D)
            for j in range(VECTOR_SUMS):
                neg_mean[c * CHUNK + j] = means[:, j : j + 1]

        def scalar_mean(c):
            means = stats.tile([P, CHUNK - VECTOR_SUMS], F32, name="neg_mean_s")
            nc.scalar.mul(out=means[:], in_=sums_s[c][:], mul=-1.0 / D)
            for j in range(VECTOR_SUMS, CHUNK):
                neg_mean[c * CHUNK + j] = means[:, j - VECTOR_SUMS : j - VECTOR_SUMS + 1]

        def squares(i):
            c, j = divmod(i, CHUNK)
            if j == 0:
                sq_sums[c] = stats.tile([P, CHUNK], F32, name="sq_sums")
            unread = scrap.tile([P, D], BF16, name="unread_s")
            nc.scalar.activation(
                out=unread[:],
                in_=x_tiles[c][:, j, :],
                func=ACT.Square,
                bias=neg_mean[i],
                scale=1.0,
                accum_out=sq_sums[c][:, j : j + 1],
            )

        std = {}

        def deviation(c):
            std[c] = stats.tile([P, CHUNK], F32, name="std")
            nc.scalar.activation(
                out=std[c][:], in_=sq_sums[c][:], func=ACT.Sqrt, bias=eps[:, 0:1], scale=1.0 / D
            )

        def inverse_deviation(c):
            rstd[c] = stats.tile([P, CHUNK], F32, name="rstd")
            nc.vector.reciprocal(out=rstd[c][:], in_=std[c][:])

        def normalise(i):
            c, j = divmod(i, CHUNK)
            y_tiles[i] = y_pool.tile([P, D], F32, name="y")
            nc.gpsimd.tensor_scalar(
                out=y_tiles[i][:],
                in0=x_tiles[c][:, j, :],
                scalar1=neg_mean[i],
                scalar2=rstd[c][:, j : j + 1],
                op0=ALU.add,
                op1=ALU.mult,
            )

        def transpose(i):
            turned[i] = []
            for g in range(PASSES):
                bank = psum_t.tile([P, PACK, P], F32, name="turned")
                for t in range(PACK):
                    k0 = g * K_PASS + t * P
                    nc.tensor.transpose(bank[:, t, :], y_tiles[i][:, k0 : k0 + P], ident_f32[:])
                turned[i].append(bank)

        def gain(i):
            c, j = divmod(i, CHUNK)
            if j == 0:
                grouped[c] = mx_pool.tile(
                    [P, CHUNK, PASSES, P, PACK], BF16, name="grouped", align_bytes=64
                )
            for g in range(PASSES):
                nc.vector.tensor_tensor(
                    out=grouped[c][:, j, g, :, :],
                    in0=turned[i][g][:].rearrange("p t r -> p r t"),
                    in1=gain_cols[:, g * PACK : (g + 1) * PACK].unsqueeze(1).to_broadcast([P, P, PACK]),
                    op=ALU.mult,
                )

        def quantise(c):
            codes[c] = mx_pool.tile([P, CHUNK, PASSES, P], U32, name="codes", align_bytes=64)
            scales[c] = mx_pool.tile([P, CHUNK, PASSES, P], U8, name="scales", align_bytes=64)
            nc.vector.quantize_mx(
                out=codes[c][:].rearrange("p j g r -> p (j g r)").bitcast(FP8X4),
                scales=scales[c][:].rearrange("p j g r -> p (j g r)"),
                in_=grouped[c][:].rearrange("p j g r t -> p (j g r t)"),
            )

        def project(c):
            for j in range(CHUNK):
                i = c * CHUNK + j
                acc[i] = psum_o.tile([P, N_PAD], F32, name="acc")
                for g in range(PASSES):
                    nc.tensor.matmul_mx(
                        out=acc[i][:],
                        lhsT=codes[c][:, j, g, :].bitcast(FP8X4),
                        lhsT_scale=scales[c][:, j, g, :],
                        rhs=w_codes[:, g, :].bitcast(FP8X4),
                        rhs_scale=w_scales[:, g, :],
                        start=(g == 0),
                        stop=(g == PASSES - 1),
                    )

        def copy_out(i):
            c, j = divmod(i, CHUNK)
            if j == 0:
                out_tiles[c] = out_pool.tile([P, 3 * HEADS, CHUNK, DH], F32, name="out_chunk")
            nc.scalar.copy(
                out=out_tiles[c][:, :, j, :],
                in_=acc[i][:, 0:C].rearrange("p (a d) -> p a d", d=DH),
            )

        def store(c):
            b, q = divmod(c, CHUNKS_PER_BATCH)
            for w in range(3):
                rows = outs[w][b].rearrange("n (p s) d -> p n s d", s=ROWS)
                nc.sync.dma_start(
                    out=rows[:, :, q * CHUNK : (q + 1) * CHUNK, :],
                    in_=out_tiles[c][:, w * HEADS : (w + 1) * HEADS, :, :],
                )

        def due(step, lag):
            c = step - lag
            return c if 0 <= c < CHUNKS else None

        for step in range(CHUNKS + QUANTISE_LAG):
            summed = due(step, 0)
            squared = due(step, SQUARES_LAG)
            normalised = due(step, NORMALISE_LAG)
            gained = due(step, GAIN_LAG)
            quantised = due(step, QUANTISE_LAG)

            if due(step, -PREFETCH) is not None:
                load(step + PREFETCH)

            if squared is not None:
                vector_mean(squared)
            if quantised == 0:
                quantise_weights()
            if quantised is not None:
                quantise(quantised)
            if normalised is not None:
                inverse_deviation(normalised)

            if quantised is not None:
                project(quantised)

            for j in range(CHUNK):
                if summed is not None:
                    row_sum(summed * CHUNK + j)
                if squared is not None:
                    squares(squared * CHUNK + j)
                if normalised is not None:
                    normalise(normalised * CHUNK + j)
                if gained is not None:
                    gain(gained * CHUNK + j)
                i = (step - GAIN_LAG) * CHUNK + j + TRANSPOSE_AHEAD
                if 0 <= i < TILES:
                    transpose(i)
                if quantised is not None:
                    copy_out(quantised * CHUNK + j)

            if summed is not None:
                scalar_mean(summed)
            if squared is not None:
                deviation(squared)
            if quantised is not None:
                store(quantised)
